import numpy as np
import ml_dtypes


def mxq(x, axis, fmt="e4m3"):
    dtype, down = {"e4m3": (ml_dtypes.float8_e4m3fn, 7), "e5m2": (ml_dtypes.float8_e5m2, 14)}[fmt]
    v = np.moveaxis(np.asarray(x, np.float32).astype(ml_dtypes.bfloat16).astype(np.float64), axis, -1)
    blocks = v.reshape(v.shape[:-1] + (-1, 32))
    amax = np.abs(blocks).max(-1, keepdims=True)
    byte = np.maximum(np.where(amax > 0, np.frexp(amax)[1] - 1 + 127, 0) - down, 1)
    scale = np.exp2(byte - 127.0)
    codes = (blocks / scale).astype(np.float32).astype(dtype).astype(np.float64)
    return np.moveaxis((codes * scale).reshape(v.shape), -1, axis)


WIDE = False


def mx_kscale(k):
    if not WIDE:
        return np.ones(k)
    levels = np.array([10, -10, 5, -5, 0])
    a = np.random.permutation(np.resize(levels, k // 512 * 4)).reshape(k // 512, 4)
    idx = np.arange(k)
    return np.exp2(a[idx // 512, idx % 128 // 32])


BF16 = ml_dtypes.bfloat16


def bf(x):
    return np.asarray(x, np.float32).astype(BF16)


def f64(x):
    return np.asarray(x).astype(np.float64)


E2M1 = np.array([0.0, 0.5, 1.0, 1.5, 2.0, 3.0, 4.0, 6.0, -0.0, -0.5, -1.0, -1.5, -2.0, -3.0, -4.0, -6.0])


def pack_weight(w, fmt):
    k, n = w.shape
    w = f64(bf(w)).reshape(k // 32, 32, n)
    amax = np.abs(w).max(1)
    if fmt == "e4m3":
        byte = np.frexp(amax)[1] - 1 + 127 - 7
    else:
        mant, ex = np.frexp(amax / 6.0)
        byte = np.where(mant > 0.5, ex, ex - 1) + 127
    byte = np.clip(np.where(amax > 0, byte, 1), 1, 254)
    scaled = (w * np.exp2(127.0 - byte)[:, None, :]).reshape(k, n).astype(np.float32)
    by_word = np.ascontiguousarray(scaled.reshape(k // 512, 128, 4, n).transpose(0, 1, 3, 2))
    if fmt == "e4m3":
        words = by_word.astype(ml_dtypes.float8_e4m3fn).view(np.uint8)
    else:
        c = by_word.astype(ml_dtypes.float4_e2m1fn).view(np.uint8) & 0xF
        words = c[..., 0::2] | (c[..., 1::2] << 4)
    return np.ascontiguousarray(words), np.ascontiguousarray(byte.astype(np.uint8).reshape(k // 512, 16, n))


def unpack_weight(words, scales, fmt):
    g, p, n, _ = words.shape
    if fmt == "e4m3":
        vals = np.ascontiguousarray(words).view(ml_dtypes.float8_e4m3fn).astype(np.float64)
    else:
        nib = np.empty((g, p, n, 4), np.uint8)
        nib[..., 0::2] = words & 0xF
        nib[..., 1::2] = words >> 4
        vals = E2M1[nib]
    vals = vals * np.repeat(np.exp2(scales.astype(np.float64) - 127.0), 8, axis=1)[..., None]
    return vals.transpose(0, 1, 3, 2).reshape(g * 512, n)

def pack4(w):
    words, scales = pack_weight(w, "e2m1")
    return words.reshape(words.shape[0], 128, -1), scales


def unpack4(words, scales):
    return unpack_weight(words.reshape(words.shape[0], 128, -1, 2), scales, "e2m1")


B, C, D, T, H, W, P = 4, 512, 256, 8, 16, 16, 2
N = T * H * W
NP = T * (H // P) * (W // P)


def conv1x1(wq, b, xq):
    return ((wq @ xq) + b[None, :, None]).reshape(B, D, T, H, W)


def maxpool(v):
    return v.reshape(B, D, T, H // P, P, W // P, P).max(axis=(4, 6))


def setup_inputs():
    s = mx_kscale(C)
    a = 1.0 / np.sqrt(C) / s[None, :]
    x = bf(np.random.standard_normal((B, C, T, H, W)) * s[None, :, None, None, None])
    g_w_words, g_w_scales = pack4(np.ascontiguousarray((np.random.standard_normal((D, C)) * 0.15 * a).T))
    g_b = bf(np.random.standard_normal(D) * 0.03)
    theta_w_words, theta_w_scales = pack4(np.ascontiguousarray((np.random.standard_normal((D, C)) * 2.0 * a).T))
    theta_b = bf(np.random.standard_normal(D) * 0.2)
    phi_w_words, phi_w_scales = pack4(np.ascontiguousarray((np.random.standard_normal((D, C)) * a).T))
    phi_b = bf(np.random.standard_normal(D) * 0.1)
    return {"x": x,
            "g_w_words": g_w_words,
            "g_w_scales": g_w_scales,
            "g_b": g_b,
            "theta_w_words": theta_w_words,
            "theta_w_scales": theta_w_scales,
            "theta_b": theta_b,
            "phi_w_words": phi_w_words,
            "phi_w_scales": phi_w_scales,
            "phi_b": phi_b}


def reference(x, g_w_words, g_w_scales, g_b, theta_w_words, theta_w_scales, theta_b, phi_w_words, phi_w_scales, phi_b):
    xq = mxq(f64(x).reshape(B, C, N), 1, "e4m3")
    g_x = maxpool(conv1x1(unpack4(g_w_words, g_w_scales).T, f64(g_b), xq)).reshape(B, D, NP)
    theta_x = conv1x1(unpack4(theta_w_words, theta_w_scales).T, f64(theta_b), xq).reshape(B, D, N)
    phi_x = maxpool(conv1x1(unpack4(phi_w_words, phi_w_scales).T, f64(phi_b), xq)).reshape(B, D, NP)
    return g_x, theta_x, phi_x

@@ -1,0 +1,204 @@
+from contextlib import ExitStack
+
+import concourse.mybir as mybir
+
+BF16 = mybir.dt.bfloat16
+F32 = mybir.dt.float32
+I32 = mybir.dt.int32
+U8 = mybir.dt.uint8
+U32 = mybir.dt.uint32
+FP8X4 = mybir.dt.float8_e4m3fn_x4
+FP4X4 = mybir.dt.float4_e2m1fn_x4
+
+P = 128
+PACK = 4
+BATCH = 4
+OUT_CHANNELS = 256
+HALVES = OUT_CHANNELS // P
+POSITIONS = 8 * 16 * 16
+UNIT = 512
+UNITS = POSITIONS // UNIT
+WIDTH = 16
+WINDOW = 2
+POOLED_WIDTH = WIDTH // WINDOW
+POOLED_UNIT = UNIT // (WINDOW * WINDOW)
+POOLED_ROWS = POOLED_UNIT // POOLED_WIDTH
+SCALE_ROWS = 4
+QUADRANTS = 4
+
+VECTOR_COLUMNS = 160
+RUN = 4
+
+THETA, G, PHI = 0, 1, 2
+
+FLOPS = 2 * BATCH * POSITIONS * (P * PACK) * (3 * OUT_CHANNELS)
+
+
+def tile_nonlocalblocknd_pa_t_kernel(
+    tc,
+    x,
+    g_w_words,
+    g_w_scales,
+    g_b,
+    theta_w_words,
+    theta_w_scales,
+    theta_b,
+    phi_w_words,
+    phi_w_scales,
+    phi_b,
+    out_0,
+    out_1,
+    out_2,
+):
+    nc = tc.nc
+    given = {
+        THETA: (theta_w_words, theta_w_scales, theta_b),
+        G: (g_w_words, g_w_scales, g_b),
+        PHI: (phi_w_words, phi_w_scales, phi_b),
+    }
+    pooled_out = {G: out_0, PHI: out_2}
+    all_units = [(b, u) for b in range(BATCH) for u in range(UNITS)]
+
+    with ExitStack() as ctx:
+        ctx.enter_context(tc.manual_schedule())
+        consts = ctx.enter_context(tc.tile_pool(name="consts", bufs=1))
+        x_first = ctx.enter_context(tc.tile_pool(name="x_first", bufs=UNITS))
+        x_rest = ctx.enter_context(tc.tile_pool(name="x_rest", bufs=BATCH - 1))
+        theta_pool = ctx.enter_context(tc.tile_pool(name="theta", bufs=len(all_units) * HALVES))
+        pooled_pool = ctx.enter_context(tc.tile_pool(name="pooled", bufs=BATCH))
+        stage = ctx.enter_context(tc.tile_pool(name="stage", bufs=4))
+        psum = ctx.enter_context(tc.psum_pool(name="psum", bufs=8))
+
+        x_rows = x.rearrange("b (p t) f h w -> b p t (f h w)", t=PACK)
+        raw = {}
+
+        def load_first_batch_unit(u):
+            x_unit = x_first.tile([P, PACK, UNIT], BF16)
+            nc.sync.dma_start(out=x_unit[:], in_=x_rows[0, :, :, u * UNIT : (u + 1) * UNIT])
+            raw[(0, u)] = x_unit[:]
+
+        w_words = consts.tile([P, 3, 2 * OUT_CHANNELS], U8, align_bytes=64)
+        w_scales = consts.tile([P, 3, OUT_CHANNELS], U8, align_bytes=64)
+        nc.vector.memset(w_scales[:].bitcast(I32), 0)
+
+        def load_weight(conv):
+            words, scales = given[conv][0], given[conv][1]
+            nc.sync.dma_start(out=w_words[:, conv, :].bitcast(I32), in_=words[0].bitcast(I32))
+            for q in range(QUADRANTS):
+                nc.sync.dma_start(
+                    out=w_scales[32 * q : 32 * q + SCALE_ROWS, conv, :].bitcast(I32),
+                    in_=scales[0, SCALE_ROWS * q : SCALE_ROWS * (q + 1), :].bitcast(I32),
+                )
+
+        for u in range(UNITS - 1):
+            load_first_batch_unit(u)
+        for conv in (THETA, G, PHI):
+            load_weight(conv)
+        load_first_batch_unit(UNITS - 1)
+        for b in range(1, BATCH):
+            x_batch = x_rest.tile([P, PACK, POSITIONS], BF16)
+            nc.sync.dma_start(out=x_batch[:], in_=x_rows[b])
+            for u in range(UNITS):
+                raw[(b, u)] = x_batch[:, :, u * UNIT : (u + 1) * UNIT]
+
+        bias = {}
+        with nc.allow_non_contiguous_dma(reason="256 bias values, one to a partition"):
+            for conv in (THETA, G, PHI):
+                bias[conv] = consts.tile([P, HALVES], BF16, name="bias_%d" % conv)
+                nc.gpsimd.dma_start(
+                    out=bias[conv][:], in_=given[conv][2].rearrange("(h p) -> p h", p=P)
+                )
+
+        grouped = {}
+        codes = {}
+        x_scales = {}
+        pooled = {}
+
+        def regroup(unit):
+            grouped[unit] = stage.tile([P, UNIT, PACK], BF16, align_bytes=64, name="grouped")
+            to_words = grouped[unit][:].rearrange("p (c i) t -> p c t i", i=RUN)
+            from_rows = raw[unit].rearrange("p t (c i) -> p c t i", i=RUN)
+            split = VECTOR_COLUMNS // RUN
+            nc.vector.tensor_copy(out=to_words[:, :split], in_=from_rows[:, :split])
+            nc.scalar.copy(out=to_words[:, split:], in_=from_rows[:, split:])
+
+        def quantise(unit):
+            codes[unit] = stage.tile([P, UNIT], U32, align_bytes=64, name="codes")
+            x_scales[unit] = stage.tile([P, UNIT], U8, align_bytes=64, name="x_scales")
+            nc.vector.quantize_mx(
+                out=codes[unit][:].bitcast(FP8X4),
+                scales=x_scales[unit][:],
+                in_=grouped[unit][:].rearrange("p n t -> p (n t)"),
+            )
+
+        def convolve(unit, conv, h):
+            bank = psum.tile([P, UNIT], F32, name="bank")
+            nc.tensor.matmul_mx(
+                out=bank[:],
+                lhsT=w_words[:, conv, 2 * P * h : 2 * P * (h + 1)].bitcast(FP4X4),
+                lhsT_scale=w_scales[:, conv, P * h : P * (h + 1)],
+                rhs=codes[unit][:].bitcast(FP8X4),
+                rhs_scale=x_scales[unit][:],
+                start=True,
+                stop=True,
+            )
+            return bank
+
+        def finish_theta(unit, h, bank):
+            b, u = unit
+            theta_sb = theta_pool.tile([P, UNIT], F32)
+            nc.scalar.activation(
+                out=theta_sb[:],
+                in_=bank[:],
+                func=mybir.ActivationFunctionType.Identity,
+                bias=bias[THETA][:, h : h + 1],
+                scale=1.0,
+            )
+            nc.sync.dma_start(
+                out=out_1[b, P * h : P * (h + 1), u * UNIT : (u + 1) * UNIT], in_=theta_sb[:]
+            )
+
+        def finish_pooled(unit, conv, h, bank):
+            b, u = unit
+            if u == 0:
+                pooled[(conv, h)] = pooled_pool.tile(
+                    [P, UNITS * POOLED_UNIT], F32, name="pooled_%d_%d" % (conv, h)
+                )
+            whole = pooled[(conv, h)]
+            nc.vector.tensor_reduce(
+                out=whole[:, u * POOLED_UNIT : (u + 1) * POOLED_UNIT].rearrange(
+                    "p (r w) -> p r w", w=POOLED_WIDTH
+                ),
+                in_=bank[:].rearrange(
+                    "p (r i w j) -> p r w i j", i=WINDOW, w=POOLED_WIDTH, j=WINDOW
+                ),
+                axis=mybir.AxisListType.XY,
+                op=mybir.AluOpType.max,
+            )
+            if u == UNITS - 1:
+                nc.scalar.activation(
+                    out=whole[:],
+                    in_=whole[:],
+                    func=mybir.ActivationFunctionType.Identity,
+                    bias=bias[conv][:, h : h + 1],
+                    scale=1.0,
+                )
+                nc.sync.dma_start(out=pooled_out[conv][b, P * h : P * (h + 1), :], in_=whole[:])
+
+        regroup(all_units[0])
+        regroup(all_units[1])
+        quantise(all_units[0])
+        for step, unit in enumerate(all_units):
+            if step + 2 < len(all_units):
+                regroup(all_units[step + 2])
+            if step + 1 < len(all_units):
+                quantise(all_units[step + 1])
+            banks = {}
+            for conv in (THETA, G, PHI):
+                for h in range(HALVES):
+                    banks[(conv, h)] = convolve(unit, conv, h)
+            for h in range(HALVES):
+                finish_theta(unit, h, banks[(THETA, h)])
+            for conv in (G, PHI):
+                for h in range(HALVES):
+                    finish_pooled(unit, conv, h, banks[(conv, h)])

@@ -26,7 +26,7 @@ POOLED_ROWS = POOLED_UNIT // POOLED_WIDTH
 SCALE_ROWS = 4
 QUADRANTS = 4
 
-VECTOR_COLUMNS = 160
+GPSIMD_COLUMNS = 288
 RUN = 4
 
 THETA, G, PHI = 0, 1, 2
@@ -90,24 +90,29 @@ def tile_nonlocalblocknd_pa_t_kernel(
                     in_=scales[0, SCALE_ROWS * q : SCALE_ROWS * (q + 1), :].bitcast(I32),
                 )
 
+        bias = {}
+
+        def load_bias(conv):
+            bias[conv] = consts.tile([P, HALVES], BF16, name="bias_%d" % conv)
+            with nc.allow_non_contiguous_dma(reason="256 bias values, one to a partition"):
+                nc.sync.dma_start(
+                    out=bias[conv][:], in_=given[conv][2].rearrange("(h p) -> p h", p=P)
+                )
+
         for u in range(UNITS - 1):
             load_first_batch_unit(u)
-        for conv in (THETA, G, PHI):
-            load_weight(conv)
+        load_weight(THETA)
+        load_bias(THETA)
+        load_weight(G)
+        load_weight(PHI)
         load_first_batch_unit(UNITS - 1)
+        load_bias(G)
+        load_bias(PHI)
         for b in range(1, BATCH):
             x_batch = x_rest.tile([P, PACK, POSITIONS], BF16)
             nc.sync.dma_start(out=x_batch[:], in_=x_rows[b])
             for u in range(UNITS):
                 raw[(b, u)] = x_batch[:, :, u * UNIT : (u + 1) * UNIT]
-
-        bias = {}
-        with nc.allow_non_contiguous_dma(reason="256 bias values, one to a partition"):
-            for conv in (THETA, G, PHI):
-                bias[conv] = consts.tile([P, HALVES], BF16, name="bias_%d" % conv)
-                nc.gpsimd.dma_start(
-                    out=bias[conv][:], in_=given[conv][2].rearrange("(h p) -> p h", p=P)
-                )
 
         grouped = {}
         codes = {}
@@ -116,11 +121,18 @@ def tile_nonlocalblocknd_pa_t_kernel(
 
         def regroup(unit):
             grouped[unit] = stage.tile([P, UNIT, PACK], BF16, align_bytes=64, name="grouped")
-            to_words = grouped[unit][:].rearrange("p (c i) t -> p c t i", i=RUN)
-            from_rows = raw[unit].rearrange("p t (c i) -> p c t i", i=RUN)
-            split = VECTOR_COLUMNS // RUN
-            nc.vector.tensor_copy(out=to_words[:, :split], in_=from_rows[:, :split])
-            nc.scalar.copy(out=to_words[:, split:], in_=from_rows[:, split:])
+            nc.gpsimd.tensor_scalar(
+                out=grouped[unit][:, :GPSIMD_COLUMNS, :],
+                in0=raw[unit][:, :, :GPSIMD_COLUMNS].rearrange("p t n -> p n t"),
+                scalar1=1.0,
+                scalar2=0.0,
+                op0=mybir.AluOpType.mult,
+                op1=mybir.AluOpType.add,
+            )
+            nc.scalar.copy(
+                out=grouped[unit][:, GPSIMD_COLUMNS:, :].rearrange("p (c i) t -> p c t i", i=RUN),
+                in_=raw[unit][:, :, GPSIMD_COLUMNS:].rearrange("p t (c i) -> p c t i", i=RUN),
+            )
 
         def quantise(unit):
             codes[unit] = stage.tile([P, UNIT], U32, align_bytes=64, name="codes")

@@ -26,8 +26,11 @@ POOLED_ROWS = POOLED_UNIT // POOLED_WIDTH
 SCALE_ROWS = 4
 QUADRANTS = 4
 
-GPSIMD_COLUMNS = 288
+HELPER_COLUMNS = 288
+VECTOR_HELPS = 3
 RUN = 4
+GROUPED_BUFFERS = 2
+UNIT_LOADS = 2
 
 THETA, G, PHI = 0, 1, 2
 
@@ -62,20 +65,27 @@ def tile_nonlocalblocknd_pa_t_kernel(
     with ExitStack() as ctx:
         ctx.enter_context(tc.manual_schedule())
         consts = ctx.enter_context(tc.tile_pool(name="consts", bufs=1))
-        x_first = ctx.enter_context(tc.tile_pool(name="x_first", bufs=UNITS))
-        x_rest = ctx.enter_context(tc.tile_pool(name="x_rest", bufs=BATCH - 1))
+        x_units = ctx.enter_context(tc.tile_pool(name="x_units", bufs=UNIT_LOADS * UNITS))
+        x_whole = ctx.enter_context(tc.tile_pool(name="x_whole", bufs=BATCH - UNIT_LOADS))
         theta_pool = ctx.enter_context(tc.tile_pool(name="theta", bufs=len(all_units) * HALVES))
         pooled_pool = ctx.enter_context(tc.tile_pool(name="pooled", bufs=BATCH))
+        grouped_pool = ctx.enter_context(tc.tile_pool(name="grouped", bufs=GROUPED_BUFFERS))
         stage = ctx.enter_context(tc.tile_pool(name="stage", bufs=4))
         psum = ctx.enter_context(tc.psum_pool(name="psum", bufs=8))
 
         x_rows = x.rearrange("b (p t) f h w -> b p t (f h w)", t=PACK)
         raw = {}
 
-        def load_first_batch_unit(u):
-            x_unit = x_first.tile([P, PACK, UNIT], BF16)
-            nc.sync.dma_start(out=x_unit[:], in_=x_rows[0, :, :, u * UNIT : (u + 1) * UNIT])
-            raw[(0, u)] = x_unit[:]
+        def load_unit(b, u):
+            x_unit = x_units.tile([P, PACK, UNIT], BF16)
+            nc.sync.dma_start(out=x_unit[:], in_=x_rows[b, :, :, u * UNIT : (u + 1) * UNIT])
+            raw[(b, u)] = x_unit[:]
+
+        def load_batch_element(b):
+            x_batch = x_whole.tile([P, PACK, POSITIONS], BF16)
+            nc.sync.dma_start(out=x_batch[:], in_=x_rows[b])
+            for u in range(UNITS):
+                raw[(b, u)] = x_batch[:, :, u * UNIT : (u + 1) * UNIT]
 
         w_words = consts.tile([P, 3, 2 * OUT_CHANNELS], U8, align_bytes=64)
         w_scales = consts.tile([P, 3, OUT_CHANNELS], U8, align_bytes=64)
@@ -99,39 +109,49 @@ def tile_nonlocalblocknd_pa_t_kernel(
                     out=bias[conv][:], in_=given[conv][2].rearrange("(h p) -> p h", p=P)
                 )
 
-        for u in range(UNITS - 1):
-            load_first_batch_unit(u)
+        load_unit(0, 0)
+        load_unit(0, 1)
+        load_unit(0, 2)
+        load_weight(G)
+        load_unit(0, 3)
         load_weight(THETA)
         load_bias(THETA)
-        load_weight(G)
+        load_unit(1, 0)
         load_weight(PHI)
-        load_first_batch_unit(UNITS - 1)
+        for u in range(1, UNITS):
+            load_unit(1, u)
         load_bias(G)
         load_bias(PHI)
-        for b in range(1, BATCH):
-            x_batch = x_rest.tile([P, PACK, POSITIONS], BF16)
-            nc.sync.dma_start(out=x_batch[:], in_=x_rows[b])
-            for u in range(UNITS):
-                raw[(b, u)] = x_batch[:, :, u * UNIT : (u + 1) * UNIT]
+        for b in range(UNIT_LOADS, BATCH):
+            load_batch_element(b)
 
         grouped = {}
         codes = {}
         x_scales = {}
         pooled = {}
 
-        def regroup(unit):
-            grouped[unit] = stage.tile([P, UNIT, PACK], BF16, align_bytes=64, name="grouped")
-            nc.gpsimd.tensor_scalar(
-                out=grouped[unit][:, :GPSIMD_COLUMNS, :],
-                in0=raw[unit][:, :, :GPSIMD_COLUMNS].rearrange("p t n -> p n t"),
-                scalar1=1.0,
-                scalar2=0.0,
-                op0=mybir.AluOpType.mult,
-                op1=mybir.AluOpType.add,
-            )
+        def regroup(step):
+            unit = all_units[step]
+            grouped[unit] = grouped_pool.tile([P, UNIT, PACK], BF16, align_bytes=64, name="grouped")
+            if step < VECTOR_HELPS:
+                nc.vector.tensor_copy(
+                    out=grouped[unit][:, :HELPER_COLUMNS, :].rearrange(
+                        "p (c i) t -> p c t i", i=RUN
+                    ),
+                    in_=raw[unit][:, :, :HELPER_COLUMNS].rearrange("p t (c i) -> p c t i", i=RUN),
+                )
+            else:
+                nc.gpsimd.tensor_scalar(
+                    out=grouped[unit][:, :HELPER_COLUMNS, :],
+                    in0=raw[unit][:, :, :HELPER_COLUMNS].rearrange("p t n -> p n t"),
+                    scalar1=1.0,
+                    scalar2=0.0,
+                    op0=mybir.AluOpType.mult,
+                    op1=mybir.AluOpType.add,
+                )
             nc.scalar.copy(
-                out=grouped[unit][:, GPSIMD_COLUMNS:, :].rearrange("p (c i) t -> p c t i", i=RUN),
-                in_=raw[unit][:, :, GPSIMD_COLUMNS:].rearrange("p t (c i) -> p c t i", i=RUN),
+                out=grouped[unit][:, HELPER_COLUMNS:, :].rearrange("p (c i) t -> p c t i", i=RUN),
+                in_=raw[unit][:, :, HELPER_COLUMNS:].rearrange("p t (c i) -> p c t i", i=RUN),
             )
 
         def quantise(unit):
@@ -197,16 +217,16 @@ def tile_nonlocalblocknd_pa_t_kernel(
                 )
                 nc.sync.dma_start(out=pooled_out[conv][b, P * h : P * (h + 1), :], in_=whole[:])
 
-        regroup(all_units[0])
-        regroup(all_units[1])
+        regroup(0)
+        regroup(1)
         quantise(all_units[0])
         for step, unit in enumerate(all_units):
             if step + 2 < len(all_units):
-                regroup(all_units[step + 2])
+                regroup(step + 2)
             if step + 1 < len(all_units):
                 quantise(all_units[step + 1])
             banks = {}
-            for conv in (THETA, G, PHI):
+            for conv in (G, THETA, PHI):
                 for h in range(HALVES):
                     banks[(conv, h)] = convolve(unit, conv, h)
             for h in range(HALVES):

@@ -16,25 +16,40 @@ BATCH = 4
 OUT_CHANNELS = 256
 HALVES = OUT_CHANNELS // P
 POSITIONS = 8 * 16 * 16
-UNIT = 512
+BANK = 512
+UNIT = 1024
 UNITS = POSITIONS // UNIT
-WIDTH = 16
 WINDOW = 2
-POOLED_WIDTH = WIDTH // WINDOW
-POOLED_UNIT = UNIT // (WINDOW * WINDOW)
-POOLED_ROWS = POOLED_UNIT // POOLED_WIDTH
+WIDTH = 16
+ROW = WIDTH * WINDOW
+ROWS = UNIT // ROW
+WINDOWS = UNIT // (WINDOW * WINDOW)
 SCALE_ROWS = 4
 QUADRANTS = 4
 
-HELPER_COLUMNS = 288
-VECTOR_HELPS = 3
-RUN = 4
-GROUPED_BUFFERS = 2
-UNIT_LOADS = 2
+HEAD_SHARES = (("vector", 40), ("scalar", 24))
+SHARES = (("gpsimd", 36), ("scalar", 18), ("vector", 10))
 
 THETA, G, PHI = 0, 1, 2
 
 FLOPS = 2 * BATCH * POSITIONS * (P * PACK) * (3 * OUT_CHANNELS)
+
+
+def cut(first_row, last_row, shares):
+    rows = last_row - first_row
+    total = sum(count for engine, count in shares)
+    runs = []
+    start = 0
+    for engine, count in shares:
+        stop = start + count * WINDOW * rows // total
+        for i in range(WINDOW):
+            a = max(start, i * rows)
+            b = min(stop, (i + 1) * rows)
+            if a < b:
+                runs.append((engine, i, first_row + a - i * rows, first_row + b - i * rows))
+        start = stop
+    assert start == WINDOW * rows
+    return runs
 
 
 def tile_nonlocalblocknd_pa_t_kernel(
@@ -60,39 +75,41 @@ def tile_nonlocalblocknd_pa_t_kernel(
         PHI: (phi_w_words, phi_w_scales, phi_b),
     }
     pooled_out = {G: out_0, PHI: out_2}
-    all_units = [(b, u) for b in range(BATCH) for u in range(UNITS)]
 
     with ExitStack() as ctx:
         ctx.enter_context(tc.manual_schedule())
         consts = ctx.enter_context(tc.tile_pool(name="consts", bufs=1))
-        x_units = ctx.enter_context(tc.tile_pool(name="x_units", bufs=UNIT_LOADS * UNITS))
-        x_whole = ctx.enter_context(tc.tile_pool(name="x_whole", bufs=BATCH - UNIT_LOADS))
-        theta_pool = ctx.enter_context(tc.tile_pool(name="theta", bufs=len(all_units) * HALVES))
-        pooled_pool = ctx.enter_context(tc.tile_pool(name="pooled", bufs=BATCH))
-        grouped_pool = ctx.enter_context(tc.tile_pool(name="grouped", bufs=GROUPED_BUFFERS))
-        stage = ctx.enter_context(tc.tile_pool(name="stage", bufs=4))
+        x_half = ctx.enter_context(tc.tile_pool(name="x_half", bufs=2))
+        x_unit = ctx.enter_context(tc.tile_pool(name="x_unit", bufs=3))
+        x_whole = ctx.enter_context(tc.tile_pool(name="x_whole", bufs=2))
+        grouped_pool = ctx.enter_context(tc.tile_pool(name="grouped", bufs=1))
+        code_pool = ctx.enter_context(tc.tile_pool(name="codes", bufs=BATCH * UNITS))
+        theta_pool = ctx.enter_context(tc.tile_pool(name="theta", bufs=8))
+        chain_pool = ctx.enter_context(tc.tile_pool(name="chain", bufs=4))
+        pooled_pool = ctx.enter_context(tc.tile_pool(name="pooled", bufs=8))
         psum = ctx.enter_context(tc.psum_pool(name="psum", bufs=8))
 
         x_rows = x.rearrange("b (p t) f h w -> b p t (f h w)", t=PACK)
         raw = {}
 
-        def load_unit(b, u):
-            x_unit = x_units.tile([P, PACK, UNIT], BF16)
-            nc.sync.dma_start(out=x_unit[:], in_=x_rows[b, :, :, u * UNIT : (u + 1) * UNIT])
-            raw[(b, u)] = x_unit[:]
-
-        def load_batch_element(b):
-            x_batch = x_whole.tile([P, PACK, POSITIONS], BF16)
-            nc.sync.dma_start(out=x_batch[:], in_=x_rows[b])
-            for u in range(UNITS):
-                raw[(b, u)] = x_batch[:, :, u * UNIT : (u + 1) * UNIT]
+        def load(pool, b, first, count):
+            x_sb = pool.tile([P, PACK, count], BF16, name="x_sb")
+            nc.sync.dma_start(out=x_sb[:], in_=x_rows[b, :, :, first : first + count])
+            for start in range(first, first + count, min(count, UNIT)):
+                v = UNITS * b + start // UNIT
+                row = (start % UNIT) // ROW
+                size = min(count, UNIT)
+                raw.setdefault(v, []).append(
+                    (row, row + size // ROW, x_sb[:, :, start - first : start - first + size])
+                )
 
         w_words = consts.tile([P, 3, 2 * OUT_CHANNELS], U8, align_bytes=64)
         w_scales = consts.tile([P, 3, OUT_CHANNELS], U8, align_bytes=64)
         nc.vector.memset(w_scales[:].bitcast(I32), 0)
+        bias = {}
 
         def load_weight(conv):
-            words, scales = given[conv][0], given[conv][1]
+            words, scales, b_vec = given[conv]
             nc.sync.dma_start(out=w_words[:, conv, :].bitcast(I32), in_=words[0].bitcast(I32))
             for q in range(QUADRANTS):
                 nc.sync.dma_start(
@@ -100,137 +117,160 @@ def tile_nonlocalblocknd_pa_t_kernel(
                     in_=scales[0, SCALE_ROWS * q : SCALE_ROWS * (q + 1), :].bitcast(I32),
                 )
 
-        bias = {}
-
         def load_bias(conv):
             bias[conv] = consts.tile([P, HALVES], BF16, name="bias_%d" % conv)
+            b_vec = given[conv][2]
             with nc.allow_non_contiguous_dma(reason="256 bias values, one to a partition"):
-                nc.sync.dma_start(
-                    out=bias[conv][:], in_=given[conv][2].rearrange("(h p) -> p h", p=P)
-                )
+                nc.sync.dma_start(out=bias[conv][:], in_=b_vec.rearrange("(h p) -> p h", p=P))
 
-        load_unit(0, 0)
-        load_unit(0, 1)
-        load_unit(0, 2)
+        for first in range(0, UNIT, UNIT // 2):
+            load(x_half, 0, first, UNIT // 2)
         load_weight(G)
-        load_unit(0, 3)
+        load(x_unit, 0, UNIT, UNIT)
+        load_bias(G)
+        load_weight(PHI)
+        load_bias(PHI)
         load_weight(THETA)
         load_bias(THETA)
-        load_unit(1, 0)
-        load_weight(PHI)
-        for u in range(1, UNITS):
-            load_unit(1, u)
-        load_bias(G)
-        load_bias(PHI)
-        for b in range(UNIT_LOADS, BATCH):
-            load_batch_element(b)
+        for u in range(UNITS):
+            load(x_unit, 1, u * UNIT, UNIT)
+        for b in range(2, BATCH):
+            load(x_whole, b, 0, POSITIONS)
 
         grouped = {}
         codes = {}
         x_scales = {}
-        pooled = {}
 
-        def regroup(step):
-            unit = all_units[step]
-            grouped[unit] = grouped_pool.tile([P, UNIT, PACK], BF16, align_bytes=64, name="grouped")
-            if step < VECTOR_HELPS:
-                nc.vector.tensor_copy(
-                    out=grouped[unit][:, :HELPER_COLUMNS, :].rearrange(
-                        "p (c i) t -> p c t i", i=RUN
-                    ),
-                    in_=raw[unit][:, :, :HELPER_COLUMNS].rearrange("p t (c i) -> p c t i", i=RUN),
+        def regroup(v, engines, shares):
+            if v not in grouped:
+                grouped[v] = grouped_pool.tile(
+                    [P, WINDOW, BANK, PACK], BF16, align_bytes=64, name="grouped"
                 )
-            else:
-                nc.gpsimd.tensor_scalar(
-                    out=grouped[unit][:, :HELPER_COLUMNS, :],
-                    in0=raw[unit][:, :, :HELPER_COLUMNS].rearrange("p t n -> p n t"),
-                    scalar1=1.0,
-                    scalar2=0.0,
-                    op0=mybir.AluOpType.mult,
-                    op1=mybir.AluOpType.add,
-                )
-            nc.scalar.copy(
-                out=grouped[unit][:, HELPER_COLUMNS:, :].rearrange("p (c i) t -> p c t i", i=RUN),
-                in_=raw[unit][:, :, HELPER_COLUMNS:].rearrange("p t (c i) -> p c t i", i=RUN),
-            )
+            for first_row, last_row, x_part in raw[v]:
+                for engine, i, a, b in cut(first_row, last_row, shares):
+                    if engine not in engines:
+                        continue
+                    src = x_part[:, :, (a - first_row) * ROW : (b - first_row) * ROW].rearrange(
+                        "p t (r i c) -> p i r c t", i=WINDOW, c=WIDTH
+                    )[:, i]
+                    dst = grouped[v][:, i, a * WIDTH : b * WIDTH, :].rearrange(
+                        "p (r c) t -> p r c t", c=WIDTH
+                    )
+                    if engine == "vector":
+                        nc.vector.tensor_copy(out=dst, in_=src)
+                    elif engine == "scalar":
+                        nc.scalar.copy(out=dst, in_=src)
+                    else:
+                        nc.gpsimd.tensor_scalar(
+                            out=dst,
+                            in0=src,
+                            scalar1=1.0,
+                            scalar2=0.0,
+                            op0=mybir.AluOpType.mult,
+                            op1=mybir.AluOpType.add,
+                        )
 
-        def quantise(unit):
-            codes[unit] = stage.tile([P, UNIT], U32, align_bytes=64, name="codes")
-            x_scales[unit] = stage.tile([P, UNIT], U8, align_bytes=64, name="x_scales")
+        def quantise(v):
+            codes[v] = code_pool.tile([P, UNIT], U32, align_bytes=64, name="codes")
+            x_scales[v] = code_pool.tile([P, UNIT], U8, align_bytes=64, name="x_scales")
             nc.vector.quantize_mx(
-                out=codes[unit][:].bitcast(FP8X4),
-                scales=x_scales[unit][:],
-                in_=grouped[unit][:].rearrange("p n t -> p (n t)"),
+                out=codes[v][:].bitcast(FP8X4),
+                scales=x_scales[v][:],
+                in_=grouped[v][:].rearrange("p i n t -> p (i n t)"),
             )
 
-        def convolve(unit, conv, h):
-            bank = psum.tile([P, UNIT], F32, name="bank")
+        def convolve(conv, h, v, i):
+            bank = psum.tile([P, BANK], F32, name="bank")
             nc.tensor.matmul_mx(
                 out=bank[:],
                 lhsT=w_words[:, conv, 2 * P * h : 2 * P * (h + 1)].bitcast(FP4X4),
                 lhsT_scale=w_scales[:, conv, P * h : P * (h + 1)],
-                rhs=codes[unit][:].bitcast(FP8X4),
-                rhs_scale=x_scales[unit][:],
+                rhs=codes[v][:, i * BANK : (i + 1) * BANK].bitcast(FP8X4),
+                rhs_scale=x_scales[v][:, i * BANK : (i + 1) * BANK],
                 start=True,
                 stop=True,
             )
             return bank
 
-        def finish_theta(unit, h, bank):
-            b, u = unit
-            theta_sb = theta_pool.tile([P, UNIT], F32)
-            nc.scalar.activation(
-                out=theta_sb[:],
-                in_=bank[:],
-                func=mybir.ActivationFunctionType.Identity,
-                bias=bias[THETA][:, h : h + 1],
-                scale=1.0,
-            )
+        def theta(v, h):
+            b, u = divmod(v, UNITS)
+            theta_sb = theta_pool.tile([P, UNIT], F32, name="theta_sb")
+            for i in range(WINDOW):
+                bank = convolve(THETA, h, v, i)
+                nc.scalar.activation(
+                    out=theta_sb[:].rearrange("p (r i c) -> p i r c", i=WINDOW, c=WIDTH)[:, i],
+                    in_=bank[:].rearrange("p (r c) -> p r c", c=WIDTH),
+                    func=mybir.ActivationFunctionType.Identity,
+                    bias=bias[THETA][:, h : h + 1],
+                    scale=1.0,
+                )
             nc.sync.dma_start(
                 out=out_1[b, P * h : P * (h + 1), u * UNIT : (u + 1) * UNIT], in_=theta_sb[:]
             )
 
-        def finish_pooled(unit, conv, h, bank):
-            b, u = unit
-            if u == 0:
-                pooled[(conv, h)] = pooled_pool.tile(
-                    [P, UNITS * POOLED_UNIT], F32, name="pooled_%d_%d" % (conv, h)
-                )
-            whole = pooled[(conv, h)]
-            nc.vector.tensor_reduce(
-                out=whole[:, u * POOLED_UNIT : (u + 1) * POOLED_UNIT].rearrange(
-                    "p (r w) -> p r w", w=POOLED_WIDTH
-                ),
-                in_=bank[:].rearrange(
-                    "p (r i w j) -> p r w i j", i=WINDOW, w=POOLED_WIDTH, j=WINDOW
-                ),
-                axis=mybir.AxisListType.XY,
-                op=mybir.AluOpType.max,
-            )
-            if u == UNITS - 1:
-                nc.scalar.activation(
-                    out=whole[:],
-                    in_=whole[:],
-                    func=mybir.ActivationFunctionType.Identity,
-                    bias=bias[conv][:, h : h + 1],
-                    scale=1.0,
-                )
-                nc.sync.dma_start(out=pooled_out[conv][b, P * h : P * (h + 1), :], in_=whole[:])
+        banks = {}
+        running = {}
+        pooled = {}
 
-        regroup(0)
-        regroup(1)
-        quantise(all_units[0])
-        for step, unit in enumerate(all_units):
-            if step + 2 < len(all_units):
-                regroup(step + 2)
-            if step + 1 < len(all_units):
-                quantise(all_units[step + 1])
-            banks = {}
-            for conv in (G, THETA, PHI):
+        def member(conv, h, i, j):
+            return banks[(conv, h, i)][:].rearrange("p (n j) -> p j n", j=WINDOW)[:, j]
+
+        def begin(v, conv):
+            for i in range(WINDOW):
                 for h in range(HALVES):
-                    banks[(conv, h)] = convolve(unit, conv, h)
+                    banks[(conv, h, i)] = convolve(conv, h, v, i)
+                    if i == 0:
+                        running[(conv, h)] = chain_pool.tile([P, WINDOWS], F32, name="first")
+                        nc.scalar.activation(
+                            out=running[(conv, h)][:],
+                            in_=member(conv, h, 0, 0),
+                            func=mybir.ActivationFunctionType.Identity,
+                            bias=bias[conv][:, h : h + 1],
+                            scale=1.0,
+                        )
+
+        def maximum(v, conv, i, j):
+            b, u = divmod(v, UNITS)
             for h in range(HALVES):
-                finish_theta(unit, h, banks[(THETA, h)])
-            for conv in (G, PHI):
-                for h in range(HALVES):
-                    finish_pooled(unit, conv, h, banks[(conv, h)])
+                if (i, j) == (WINDOW - 1, WINDOW - 1):
+                    if u == 0:
+                        pooled[(conv, h)] = pooled_pool.tile([P, UNITS * WINDOWS], F32, name="pooled")
+                    larger = pooled[(conv, h)][:, u * WINDOWS : (u + 1) * WINDOWS]
+                else:
+                    larger = chain_pool.tile([P, WINDOWS], F32, name="larger_%d%d" % (i, j))[:]
+                nc.vector.scalar_tensor_tensor(
+                    out=larger,
+                    in0=member(conv, h, i, j),
+                    scalar=bias[conv][:, h : h + 1],
+                    in1=running[(conv, h)][:],
+                    op0=mybir.AluOpType.add,
+                    op1=mybir.AluOpType.max,
+                )
+                running[(conv, h)] = larger
+                if (i, j) == (WINDOW - 1, WINDOW - 1) and u == UNITS - 1:
+                    nc.sync.dma_start(
+                        out=pooled_out[conv][b, P * h : P * (h + 1), :], in_=pooled[(conv, h)][:]
+                    )
+
+        last = BATCH * UNITS - 1
+        regroup(0, ("vector", "scalar"), HEAD_SHARES)
+        quantise(0)
+        for v in range(last + 1):
+            if v < last:
+                regroup(v + 1, ("gpsimd",), SHARES)
+            begin(v, G)
+            if v < last:
+                regroup(v + 1, ("scalar",), SHARES)
+            maximum(v, G, 0, 1)
+            maximum(v, G, 1, 0)
+            maximum(v, G, 1, 1)
+            begin(v, PHI)
+            if v < last:
+                regroup(v + 1, ("vector",), SHARES)
+            maximum(v, PHI, 0, 1)
+            if v < last:
+                quantise(v + 1)
+            maximum(v, PHI, 1, 0)
+            maximum(v, PHI, 1, 1)
+            theta(v, 0)
+            theta(v, 1)

@@ -28,7 +28,7 @@ SCALE_ROWS = 4
 QUADRANTS = 4
 
 HEAD_SHARES = (("vector", 40), ("scalar", 24))
-SHARES = (("gpsimd", 36), ("scalar", 18), ("vector", 10))
+SHARES = (("vector", 10), ("gpsimd", 36), ("scalar", 18))
 
 THETA, G, PHI = 0, 1, 2
 
@@ -147,9 +147,12 @@ def tile_nonlocalblocknd_pa_t_kernel(
                     [P, WINDOW, BANK, PACK], BF16, align_bytes=64, name="grouped"
                 )
             for first_row, last_row, x_part in raw[v]:
-                for engine, i, a, b in cut(first_row, last_row, shares):
+                runs = cut(first_row, last_row, shares)
+                for n, (engine, i, a, b) in enumerate(runs):
                     if engine not in engines:
                         continue
+                    if engine == "gpsimd" and n > 0 and runs[n - 1][0] == "vector":
+                        a -= 1
                     src = x_part[:, :, (a - first_row) * ROW : (b - first_row) * ROW].rearrange(
                         "p t (r i c) -> p i r c t", i=WINDOW, c=WIDTH
                     )[:, i]
@@ -247,7 +250,12 @@ def tile_nonlocalblocknd_pa_t_kernel(
                     op1=mybir.AluOpType.max,
                 )
                 running[(conv, h)] = larger
-                if (i, j) == (WINDOW - 1, WINDOW - 1) and u == UNITS - 1:
+                if (i, j) == (WINDOW - 1, WINDOW - 1) and b == BATCH - 1:
+                    nc.sync.dma_start(
+                        out=pooled_out[conv][b, P * h : P * (h + 1), u * WINDOWS : (u + 1) * WINDOWS],
+                        in_=larger,
+                    )
+                elif (i, j) == (WINDOW - 1, WINDOW - 1) and u == UNITS - 1:
                     nc.sync.dma_start(
                         out=pooled_out[conv][b, P * h : P * (h + 1), :], in_=pooled[(conv, h)][:]
                     )
@@ -255,22 +263,33 @@ def tile_nonlocalblocknd_pa_t_kernel(
         last = BATCH * UNITS - 1
         regroup(0, ("vector", "scalar"), HEAD_SHARES)
         quantise(0)
-        for v in range(last + 1):
-            if v < last:
-                regroup(v + 1, ("gpsimd",), SHARES)
+        for v in range(last):
+            regroup(v + 1, ("vector",), SHARES)
+            regroup(v + 1, ("gpsimd",), SHARES)
+            if v > 0:
+                maximum(v - 1, PHI, 1, 0)
+                maximum(v - 1, PHI, 1, 1)
+                theta(v - 1, 0)
+                theta(v - 1, 1)
             begin(v, G)
-            if v < last:
-                regroup(v + 1, ("scalar",), SHARES)
+            regroup(v + 1, ("scalar",), SHARES)
             maximum(v, G, 0, 1)
             maximum(v, G, 1, 0)
             maximum(v, G, 1, 1)
             begin(v, PHI)
-            if v < last:
-                regroup(v + 1, ("vector",), SHARES)
             maximum(v, PHI, 0, 1)
-            if v < last:
-                quantise(v + 1)
-            maximum(v, PHI, 1, 0)
-            maximum(v, PHI, 1, 1)
-            theta(v, 0)
-            theta(v, 1)
+            quantise(v + 1)
+        maximum(last - 1, PHI, 1, 0)
+        maximum(last - 1, PHI, 1, 1)
+        theta(last - 1, 0)
+        theta(last - 1, 1)
+        begin(last, G)
+        theta(last, 0)
+        maximum(last, G, 0, 1)
+        maximum(last, G, 1, 0)
+        maximum(last, G, 1, 1)
+        begin(last, PHI)
+        theta(last, 1)
+        maximum(last, PHI, 0, 1)
+        maximum(last, PHI, 1, 0)
+        maximum(last, PHI, 1, 1)

@@ -28,7 +28,7 @@ SCALE_ROWS = 4
 QUADRANTS = 4
 
 HEAD_SHARES = (("vector", 40), ("scalar", 24))
-SHARES = (("vector", 10), ("gpsimd", 36), ("scalar", 18))
+SHARES = (("gpsimd", 44), ("scalar", 20))
 
 THETA, G, PHI = 0, 1, 2
 

@@ -30,6 +30,7 @@ QUADRANTS = 4
 HEAD_SHARES = (("vector", 40), ("scalar", 24))
 SHARES = (("gpsimd", 44), ("scalar", 20))
 
+HEAD_LOADS = 4
 THETA, G, PHI = 0, 1, 2
 
 FLOPS = 2 * BATCH * POSITIONS * (P * PACK) * (3 * OUT_CHANNELS)
@@ -79,7 +80,7 @@ def tile_nonlocalblocknd_pa_t_kernel(
     with ExitStack() as ctx:
         ctx.enter_context(tc.manual_schedule())
         consts = ctx.enter_context(tc.tile_pool(name="consts", bufs=1))
-        x_half = ctx.enter_context(tc.tile_pool(name="x_half", bufs=2))
+        x_half = ctx.enter_context(tc.tile_pool(name="x_half", bufs=HEAD_LOADS))
         x_unit = ctx.enter_context(tc.tile_pool(name="x_unit", bufs=3))
         x_whole = ctx.enter_context(tc.tile_pool(name="x_whole", bufs=2))
         grouped_pool = ctx.enter_context(tc.tile_pool(name="grouped", bufs=1))
@@ -123,8 +124,8 @@ def tile_nonlocalblocknd_pa_t_kernel(
             with nc.allow_non_contiguous_dma(reason="256 bias values, one to a partition"):
                 nc.sync.dma_start(out=bias[conv][:], in_=b_vec.rearrange("(h p) -> p h", p=P))
 
-        for first in range(0, UNIT, UNIT // 2):
-            load(x_half, 0, first, UNIT // 2)
+        for first in range(0, UNIT, UNIT // HEAD_LOADS):
+            load(x_half, 0, first, UNIT // HEAD_LOADS)
         load_weight(G)
         load(x_unit, 0, UNIT, UNIT)
         load_bias(G)
@@ -173,14 +174,18 @@ def tile_nonlocalblocknd_pa_t_kernel(
                             op1=mybir.AluOpType.add,
                         )
 
-        def quantise(v):
+        def quantise(v, calls=1):
             codes[v] = code_pool.tile([P, UNIT], U32, align_bytes=64, name="codes")
             x_scales[v] = code_pool.tile([P, UNIT], U8, align_bytes=64, name="x_scales")
-            nc.vector.quantize_mx(
-                out=codes[v][:].bitcast(FP8X4),
-                scales=x_scales[v][:],
-                in_=grouped[v][:].rearrange("p i n t -> p (i n t)"),
-            )
+            width = UNIT // calls
+            for n in range(calls):
+                nc.vector.quantize_mx(
+                    out=codes[v][:, n * width : (n + 1) * width].bitcast(FP8X4),
+                    scales=x_scales[v][:, n * width : (n + 1) * width],
+                    in_=grouped[v][:].rearrange("p i n t -> p (i n t)")[
+                        :, n * width * PACK : (n + 1) * width * PACK
+                    ],
+                )
 
         def convolve(conv, h, v, i):
             bank = psum.tile([P, BANK], F32, name="bank")
@@ -262,7 +267,7 @@ def tile_nonlocalblocknd_pa_t_kernel(
 
         last = BATCH * UNITS - 1
         regroup(0, ("vector", "scalar"), HEAD_SHARES)
-        quantise(0)
+        quantise(0, WINDOW)
         for v in range(last):
             regroup(v + 1, ("vector",), SHARES)
             regroup(v + 1, ("gpsimd",), SHARES)

@@ -27,10 +27,10 @@ WINDOWS = UNIT // (WINDOW * WINDOW)
 SCALE_ROWS = 4
 QUADRANTS = 4
 
-HEAD_SHARES = (("vector", 40), ("scalar", 24))
-SHARES = (("gpsimd", 44), ("scalar", 20))
+HEAD_SHARES = (("vector", 5), ("scalar", 3))
+SHARES = (("gpsimd", 22), ("scalar", 10))
 
-HEAD_LOADS = 4
+HEAD_LOADS = 2
 THETA, G, PHI = 0, 1, 2
 
 FLOPS = 2 * BATCH * POSITIONS * (P * PACK) * (3 * OUT_CHANNELS)
@@ -40,16 +40,11 @@ def cut(first_row, last_row, shares):
     rows = last_row - first_row
     total = sum(count for engine, count in shares)
     runs = []
-    start = 0
+    start = first_row
     for engine, count in shares:
-        stop = start + count * WINDOW * rows // total
-        for i in range(WINDOW):
-            a = max(start, i * rows)
-            b = min(stop, (i + 1) * rows)
-            if a < b:
-                runs.append((engine, i, first_row + a - i * rows, first_row + b - i * rows))
-        start = stop
-    assert start == WINDOW * rows
+        runs.append((engine, start, start + count * rows // total))
+        start += count * rows // total
+    assert start == last_row
     return runs
 
 
@@ -148,17 +143,14 @@ def tile_nonlocalblocknd_pa_t_kernel(
                     [P, WINDOW, BANK, PACK], BF16, align_bytes=64, name="grouped"
                 )
             for first_row, last_row, x_part in raw[v]:
-                runs = cut(first_row, last_row, shares)
-                for n, (engine, i, a, b) in enumerate(runs):
+                for engine, a, b in cut(first_row, last_row, shares):
                     if engine not in engines:
                         continue
-                    if engine == "gpsimd" and n > 0 and runs[n - 1][0] == "vector":
-                        a -= 1
                     src = x_part[:, :, (a - first_row) * ROW : (b - first_row) * ROW].rearrange(
-                        "p t (r i c) -> p i r c t", i=WINDOW, c=WIDTH
-                    )[:, i]
-                    dst = grouped[v][:, i, a * WIDTH : b * WIDTH, :].rearrange(
-                        "p (r c) t -> p r c t", c=WIDTH
+                        "p t (r i c) -> p r i c t", i=WINDOW, c=WIDTH
+                    )
+                    dst = grouped[v][:, :, a * WIDTH : b * WIDTH, :].rearrange(
+                        "p i (r c) t -> p r i c t", c=WIDTH
                     )
                     if engine == "vector":
                         nc.vector.tensor_copy(out=dst, in_=src)

from contextlib import ExitStack

import concourse.mybir as mybir

BF16 = mybir.dt.bfloat16
F32 = mybir.dt.float32
I32 = mybir.dt.int32
U8 = mybir.dt.uint8
U32 = mybir.dt.uint32
FP8X4 = mybir.dt.float8_e4m3fn_x4
FP4X4 = mybir.dt.float4_e2m1fn_x4

P = 128
PACK = 4
BATCH = 4
OUT_CHANNELS = 256
HALVES = OUT_CHANNELS // P
POSITIONS = 8 * 16 * 16
BANK = 512
UNIT = 1024
UNITS = POSITIONS // UNIT
WINDOW = 2
WIDTH = 16
ROW = WIDTH * WINDOW
ROWS = UNIT // ROW
WINDOWS = UNIT // (WINDOW * WINDOW)
SCALE_ROWS = 4
QUADRANTS = 4

HEAD_SHARES = (("vector", 5), ("scalar", 3))
SHARES = (("gpsimd", 22), ("scalar", 10))

HEAD_LOADS = 2
THETA, G, PHI = 0, 1, 2

FLOPS = 2 * BATCH * POSITIONS * (P * PACK) * (3 * OUT_CHANNELS)


def cut(first_row, last_row, shares):
    rows = last_row - first_row
    total = sum(count for engine, count in shares)
    runs = []
    start = first_row
    for engine, count in shares:
        runs.append((engine, start, start + count * rows // total))
        start += count * rows // total
    assert start == last_row
    return runs


def tile_nonlocalblocknd_pa_t_kernel(
    tc,
    x,
    g_w_words,
    g_w_scales,
    g_b,
    theta_w_words,
    theta_w_scales,
    theta_b,
    phi_w_words,
    phi_w_scales,
    phi_b,
    out_0,
    out_1,
    out_2,
):
    nc = tc.nc
    given = {
        THETA: (theta_w_words, theta_w_scales, theta_b),
        G: (g_w_words, g_w_scales, g_b),
        PHI: (phi_w_words, phi_w_scales, phi_b),
    }
    pooled_out = {G: out_0, PHI: out_2}

    with ExitStack() as ctx:
        ctx.enter_context(tc.manual_schedule())
        consts = ctx.enter_context(tc.tile_pool(name="consts", bufs=1))
        x_half = ctx.enter_context(tc.tile_pool(name="x_half", bufs=HEAD_LOADS))
        x_unit = ctx.enter_context(tc.tile_pool(name="x_unit", bufs=3))
        x_whole = ctx.enter_context(tc.tile_pool(name="x_whole", bufs=2))
        grouped_pool = ctx.enter_context(tc.tile_pool(name="grouped", bufs=1))
        code_pool = ctx.enter_context(tc.tile_pool(name="codes", bufs=BATCH * UNITS))
        theta_pool = ctx.enter_context(tc.tile_pool(name="theta", bufs=8))
        chain_pool = ctx.enter_context(tc.tile_pool(name="chain", bufs=4))
        pooled_pool = ctx.enter_context(tc.tile_pool(name="pooled", bufs=8))
        psum = ctx.enter_context(tc.psum_pool(name="psum", bufs=8))

        x_rows = x.rearrange("b (p t) f h w -> b p t (f h w)", t=PACK)
        raw = {}

        def load(pool, b, first, count):
            x_sb = pool.tile([P, PACK, count], BF16, name="x_sb")
            nc.sync.dma_start(out=x_sb[:], in_=x_rows[b, :, :, first : first + count])
            for start in range(first, first + count, min(count, UNIT)):
                v = UNITS * b + start // UNIT
                row = (start % UNIT) // ROW
                size = min(count, UNIT)
                raw.setdefault(v, []).append(
                    (row, row + size // ROW, x_sb[:, :, start - first : start - first + size])
                )

        w_words = consts.tile([P, 3, 2 * OUT_CHANNELS], U8, align_bytes=64)
        w_scales = consts.tile([P, 3, OUT_CHANNELS], U8, align_bytes=64)
        nc.vector.memset(w_scales[:].bitcast(I32), 0)
        bias = {}

        def load_weight(conv):
            words, scales, b_vec = given[conv]
            nc.sync.dma_start(out=w_words[:, conv, :].bitcast(I32), in_=words[0].bitcast(I32))
            for q in range(QUADRANTS):
                nc.sync.dma_start(
                    out=w_scales[32 * q : 32 * q + SCALE_ROWS, conv, :].bitcast(I32),
                    in_=scales[0, SCALE_ROWS * q : SCALE_ROWS * (q + 1), :].bitcast(I32),
                )

        def load_bias(conv):
            bias[conv] = consts.tile([P, HALVES], BF16, name="bias_%d" % conv)
            b_vec = given[conv][2]
            with nc.allow_non_contiguous_dma(reason="256 bias values, one to a partition"):
                nc.sync.dma_start(out=bias[conv][:], in_=b_vec.rearrange("(h p) -> p h", p=P))

        for first in range(0, UNIT, UNIT // HEAD_LOADS):
            load(x_half, 0, first, UNIT // HEAD_LOADS)
        load_weight(G)
        load(x_unit, 0, UNIT, UNIT)
        load_bias(G)
        load_weight(PHI)
        load_bias(PHI)
        load_weight(THETA)
        load_bias(THETA)
        for u in range(UNITS):
            load(x_unit, 1, u * UNIT, UNIT)
        for b in range(2, BATCH):
            load(x_whole, b, 0, POSITIONS)

        grouped = {}
        codes = {}
        x_scales = {}

        def regroup(v, engines, shares):
            if v not in grouped:
                grouped[v] = grouped_pool.tile(
                    [P, WINDOW, BANK, PACK], BF16, align_bytes=64, name="grouped"
                )
            for first_row, last_row, x_part in raw[v]:
                for engine, a, b in cut(first_row, last_row, shares):
                    if engine not in engines:
                        continue
                    src = x_part[:, :, (a - first_row) * ROW : (b - first_row) * ROW].rearrange(
                        "p t (r i c) -> p r i c t", i=WINDOW, c=WIDTH
                    )
                    dst = grouped[v][:, :, a * WIDTH : b * WIDTH, :].rearrange(
                        "p i (r c) t -> p r i c t", c=WIDTH
                    )
                    if engine == "vector":
                        nc.vector.tensor_copy(out=dst, in_=src)
                    elif engine == "scalar":
                        nc.scalar.copy(out=dst, in_=src)
                    else:
                        nc.gpsimd.tensor_scalar(
                            out=dst,
                            in0=src,
                            scalar1=1.0,
                            scalar2=0.0,
                            op0=mybir.AluOpType.mult,
                            op1=mybir.AluOpType.add,
                        )

        def quantise(v, calls=1):
            codes[v] = code_pool.tile([P, UNIT], U32, align_bytes=64, name="codes")
            x_scales[v] = code_pool.tile([P, UNIT], U8, align_bytes=64, name="x_scales")
            width = UNIT // calls
            for n in range(calls):
                nc.vector.quantize_mx(
                    out=codes[v][:, n * width : (n + 1) * width].bitcast(FP8X4),
                    scales=x_scales[v][:, n * width : (n + 1) * width],
                    in_=grouped[v][:].rearrange("p i n t -> p (i n t)")[
                        :, n * width * PACK : (n + 1) * width * PACK
                    ],
                )

        def convolve(conv, h, v, i):
            bank = psum.tile([P, BANK], F32, name="bank")
            nc.tensor.matmul_mx(
                out=bank[:],
                lhsT=w_words[:, conv, 2 * P * h : 2 * P * (h + 1)].bitcast(FP4X4),
                lhsT_scale=w_scales[:, conv, P * h : P * (h + 1)],
                rhs=codes[v][:, i * BANK : (i + 1) * BANK].bitcast(FP8X4),
                rhs_scale=x_scales[v][:, i * BANK : (i + 1) * BANK],
                start=True,
                stop=True,
            )
            return bank

        def theta(v, h):
            b, u = divmod(v, UNITS)
            theta_sb = theta_pool.tile([P, UNIT], F32, name="theta_sb")
            for i in range(WINDOW):
                bank = convolve(THETA, h, v, i)
                nc.scalar.activation(
                    out=theta_sb[:].rearrange("p (r i c) -> p i r c", i=WINDOW, c=WIDTH)[:, i],
                    in_=bank[:].rearrange("p (r c) -> p r c", c=WIDTH),
                    func=mybir.ActivationFunctionType.Identity,
                    bias=bias[THETA][:, h : h + 1],
                    scale=1.0,
                )
            nc.sync.dma_start(
                out=out_1[b, P * h : P * (h + 1), u * UNIT : (u + 1) * UNIT], in_=theta_sb[:]
            )

        banks = {}
        running = {}
        pooled = {}

        def member(conv, h, i, j):
            return banks[(conv, h, i)][:].rearrange("p (n j) -> p j n", j=WINDOW)[:, j]

        def begin(v, conv):
            for i in range(WINDOW):
                for h in range(HALVES):
                    banks[(conv, h, i)] = convolve(conv, h, v, i)
                    if i == 0:
                        running[(conv, h)] = chain_pool.tile([P, WINDOWS], F32, name="first")
                        nc.scalar.activation(
                            out=running[(conv, h)][:],
                            in_=member(conv, h, 0, 0),
                            func=mybir.ActivationFunctionType.Identity,
                            bias=bias[conv][:, h : h + 1],
                            scale=1.0,
                        )

        def maximum(v, conv, i, j):
            b, u = divmod(v, UNITS)
            for h in range(HALVES):
                if (i, j) == (WINDOW - 1, WINDOW - 1):
                    if u == 0:
                        pooled[(conv, h)] = pooled_pool.tile([P, UNITS * WINDOWS], F32, name="pooled")
                    larger = pooled[(conv, h)][:, u * WINDOWS : (u + 1) * WINDOWS]
                else:
                    larger = chain_pool.tile([P, WINDOWS], F32, name="larger_%d%d" % (i, j))[:]
                nc.vector.scalar_tensor_tensor(
                    out=larger,
                    in0=member(conv, h, i, j),
                    scalar=bias[conv][:, h : h + 1],
                    in1=running[(conv, h)][:],
                    op0=mybir.AluOpType.add,
                    op1=mybir.AluOpType.max,
                )
                running[(conv, h)] = larger
                if (i, j) == (WINDOW - 1, WINDOW - 1) and b == BATCH - 1:
                    nc.sync.dma_start(
                        out=pooled_out[conv][b, P * h : P * (h + 1), u * WINDOWS : (u + 1) * WINDOWS],
                        in_=larger,
                    )
                elif (i, j) == (WINDOW - 1, WINDOW - 1) and u == UNITS - 1:
                    nc.sync.dma_start(
                        out=pooled_out[conv][b, P * h : P * (h + 1), :], in_=pooled[(conv, h)][:]
                    )

        last = BATCH * UNITS - 1
        regroup(0, ("vector", "scalar"), HEAD_SHARES)
        quantise(0, WINDOW)
        for v in range(last):
            regroup(v + 1, ("vector",), SHARES)
            regroup(v + 1, ("gpsimd",), SHARES)
            if v > 0:
                maximum(v - 1, PHI, 1, 0)
                maximum(v - 1, PHI, 1, 1)
                theta(v - 1, 0)
                theta(v - 1, 1)
            begin(v, G)
            regroup(v + 1, ("scalar",), SHARES)
            maximum(v, G, 0, 1)
            maximum(v, G, 1, 0)
            maximum(v, G, 1, 1)
            begin(v, PHI)
            maximum(v, PHI, 0, 1)
            quantise(v + 1)
        maximum(last - 1, PHI, 1, 0)
        maximum(last - 1, PHI, 1, 1)
        theta(last - 1, 0)
        theta(last - 1, 1)
        begin(last, G)
        theta(last, 0)
        maximum(last, G, 0, 1)
        maximum(last, G, 1, 0)
        maximum(last, G, 1, 1)
        begin(last, PHI)
        theta(last, 1)
        maximum(last, PHI, 0, 1)
        maximum(last, PHI, 1, 0)
        maximum(last, PHI, 1, 1)
